import numpy as np
import ml_dtypes


def mxq(x, axis, fmt="e4m3"):
    dtype, down = {"e4m3": (ml_dtypes.float8_e4m3fn, 7), "e5m2": (ml_dtypes.float8_e5m2, 14)}[fmt]
    v = np.moveaxis(np.asarray(x, np.float32).astype(ml_dtypes.bfloat16).astype(np.float64), axis, -1)
    blocks = v.reshape(v.shape[:-1] + (-1, 32))
    amax = np.abs(blocks).max(-1, keepdims=True)
    byte = np.maximum(np.where(amax > 0, np.frexp(amax)[1] - 1 + 127, 0) - down, 1)
    scale = np.exp2(byte - 127.0)
    codes = (blocks / scale).astype(np.float32).astype(dtype).astype(np.float64)
    return np.moveaxis((codes * scale).reshape(v.shape), -1, axis)


WIDE = False


def mx_kscale(k):
    if not WIDE:
        return np.ones(k)
    levels = np.array([10, -10, 5, -5, 0])
    a = np.random.permutation(np.resize(levels, k // 512 * 4)).reshape(k // 512, 4)
    idx = np.arange(k)
    return np.exp2(a[idx // 512, idx % 128 // 32])


BF16 = ml_dtypes.bfloat16


def bf(x):
    return np.asarray(x, np.float32).astype(BF16)


def f64(x):
    return np.asarray(x).astype(np.float64)


E2M1 = np.array([0.0, 0.5, 1.0, 1.5, 2.0, 3.0, 4.0, 6.0, -0.0, -0.5, -1.0, -1.5, -2.0, -3.0, -4.0, -6.0])


def pack_weight(w, fmt):
    k, n = w.shape
    w = f64(bf(w)).reshape(k // 32, 32, n)
    amax = np.abs(w).max(1)
    if fmt == "e4m3":
        byte = np.frexp(amax)[1] - 1 + 127 - 7
    else:
        mant, ex = np.frexp(amax / 6.0)
        byte = np.where(mant > 0.5, ex, ex - 1) + 127
    byte = np.clip(np.where(amax > 0, byte, 1), 1, 254)
    scaled = (w * np.exp2(127.0 - byte)[:, None, :]).reshape(k, n).astype(np.float32)
    by_word = np.ascontiguousarray(scaled.reshape(k // 512, 128, 4, n).transpose(0, 1, 3, 2))
    if fmt == "e4m3":
        words = by_word.astype(ml_dtypes.float8_e4m3fn).view(np.uint8)
    else:
        c = by_word.astype(ml_dtypes.float4_e2m1fn).view(np.uint8) & 0xF
        words = c[..., 0::2] | (c[..., 1::2] << 4)
    return np.ascontiguousarray(words), np.ascontiguousarray(byte.astype(np.uint8).reshape(k // 512, 16, n))


def unpack_weight(words, scales, fmt):
    g, p, n, _ = words.shape
    if fmt == "e4m3":
        vals = np.ascontiguousarray(words).view(ml_dtypes.float8_e4m3fn).astype(np.float64)
    else:
        nib = np.empty((g, p, n, 4), np.uint8)
        nib[..., 0::2] = words & 0xF
        nib[..., 1::2] = words >> 4
        vals = E2M1[nib]
    vals = vals * np.repeat(np.exp2(scales.astype(np.float64) - 127.0), 8, axis=1)[..., None]
    return vals.transpose(0, 1, 3, 2).reshape(g * 512, n)


B, S, A, O, H, L = 128, 1024, 128, 1920, 1024, 8064
G = L + A


def sigmoid(v):
    return 1.0 / (1.0 + np.exp(-v))


def setup_inputs():
    s = mx_kscale(G)
    sample = bf(np.random.standard_normal((B, L)) * 1.1 * s[:L])
    prev_action = bf(np.random.standard_normal((B, A)) * s[L:])
    prev_state = bf(np.random.standard_normal((B, S)))
    wih = np.random.standard_normal((3 * H, G)) / np.sqrt(G) / s
    whh = np.random.standard_normal((3 * H, H)) / np.sqrt(H)
    gru_bih = bf(np.random.standard_normal(3 * H) * 0.1)
    gru_bhh = bf(np.random.standard_normal(3 * H) * 0.1)
    wih_words, wih_scales = pack_weight(np.ascontiguousarray(wih.T), "e4m3")
    whh_words, whh_scales = pack_weight(np.ascontiguousarray(whh.T), "e4m3")
    return {"sample": sample,
            "prev_action": prev_action,
            "prev_state": prev_state,
            "gru_Wih_words": wih_words,
            "gru_Wih_scales": wih_scales,
            "gru_Whh_words": whh_words,
            "gru_Whh_scales": whh_scales,
            "gru_bih": gru_bih,
            "gru_bhh": gru_bhh}


def reference(sample, prev_action, prev_state, gru_Wih_words, gru_Wih_scales, gru_Whh_words, gru_Whh_scales, gru_bih, gru_bhh):
    hp = f64(prev_state)
    xg = np.concatenate([f64(sample), f64(prev_action)], axis=-1)
    gi = (mxq(xg, 1, "e4m3") @ unpack_weight(gru_Wih_words, gru_Wih_scales, "e4m3")) + f64(gru_bih)
    gh = (mxq(hp, 1, "e4m3") @ unpack_weight(gru_Whh_words, gru_Whh_scales, "e4m3")) + f64(gru_bhh)
    gi_r, gi_z, gi_n = np.split(gi, 3, axis=-1)
    gh_r, gh_z, gh_n = np.split(gh, 3, axis=-1)
    r = sigmoid(gi_r + gh_r)
    z = sigmoid(gi_z + gh_z)
    n = np.tanh(gi_n + r * gh_n)
    belief = (1.0 - z) * n + z * hp
    return belief

@@ -1,0 +1,272 @@
+from contextlib import ExitStack
+
+import concourse.mybir as mybir
+from concourse.masks import make_identity
+
+F32 = mybir.dt.float32
+BF16 = mybir.dt.bfloat16
+I32 = mybir.dt.int32
+U32 = mybir.dt.uint32
+U8 = mybir.dt.uint8
+FP8X4 = mybir.dt.float8_e4m3fn_x4
+ACT = mybir.ActivationFunctionType
+ALU = mybir.AluOpType
+
+P = 128
+PACK = 4
+K_PASS = P * PACK
+BANK = 512
+H = 1024
+GATES = 3
+SAMPLE = 8064
+STATE_GROUPS = 2
+INPUT_GROUPS = 16
+GROUPS = STATE_GROUPS + INPUT_GROUPS
+X_COLS = GROUPS * K_PASS
+X_PIECE = 2048
+PLANES_PER_TILE = 4
+QUADRANT = 32
+GROUP_WORDS = K_PASS // 2
+ROUND_GROUPS = 2
+
+FLOPS = 2 * P * GROUPS * K_PASS * GATES * H
+
+
+def load_planes(nc, planes, scales):
+    groups = scales.shape[0]
+    for quadrant in range(P // QUADRANT):
+        first = QUADRANT * quadrant
+        nc.sync.dma_start(
+            out=planes[first : first + PACK * groups, :].bitcast(I32),
+            in_=scales[:, PACK * quadrant : PACK * (quadrant + 1), :].bitcast(I32),
+        )
+
+
+def tile_rssm_pb_k_kernel(
+    tc,
+    sample,
+    prev_action,
+    prev_state,
+    gru_Wih_words,
+    gru_Wih_scales,
+    gru_Whh_words,
+    gru_Whh_scales,
+    gru_bih,
+    gru_bhh,
+    out,
+):
+    nc = tc.nc
+    with ExitStack() as ctx:
+        ctx.enter_context(tc.manual_schedule())
+        keep = ctx.enter_context(tc.tile_pool(name="keep", bufs=1))
+        stage = ctx.enter_context(tc.tile_pool(name="stage", bufs=3))
+        w_state = ctx.enter_context(tc.tile_pool(name="w_state", bufs=2))
+        w_gates = ctx.enter_context(tc.tile_pool(name="w_gates", bufs=6))
+        w_cand = ctx.enter_context(tc.tile_pool(name="w_cand", bufs=8))
+        psum_rz = ctx.enter_context(tc.psum_pool(name="psum_rz", bufs=1))
+        psum_work = ctx.enter_context(tc.psum_pool(name="psum_work", bufs=4))
+
+        bias_rows = keep.tile([P, (GATES + 1) * H], BF16)
+        nc.vector.memset(bias_rows[:], 0.0)
+        ones = keep.tile([P, P], BF16)
+        nc.vector.memset(ones[:], 1.0)
+        identity = keep.tile([P, P], F32)
+        make_identity(nc, identity[:])
+        state_planes = keep.tile([P, GATES * H], U8, align_bytes=64)
+        nc.vector.memset(state_planes[:].bitcast(I32), 0)
+        input_planes = []
+        for j in range(INPUT_GROUPS // PLANES_PER_TILE):
+            planes = keep.tile([P, GATES * H], U8, name="input_planes%d" % j, align_bytes=64)
+            nc.vector.memset(planes[:].bitcast(I32), 0)
+            input_planes.append(planes)
+
+        x_sb = keep.tile([P, X_COLS], BF16)
+        nc.sync.dma_start(out=x_sb[:, 0:H], in_=prev_state)
+        for first in range(0, SAMPLE, X_PIECE):
+            last = min(first + X_PIECE, SAMPLE)
+            nc.sync.dma_start(out=x_sb[:, H + first : H + last], in_=sample[:, first:last])
+        nc.sync.dma_start(out=x_sb[:, H + SAMPLE : X_COLS], in_=prev_action)
+
+        bih = gru_bih.rearrange("(o n) -> o n", o=1)
+        bhh = gru_bhh.rearrange("(o n) -> o n", o=1)
+        nc.sync.dma_start(out=bias_rows[0:1, 0 : 3 * H], in_=bih)
+        nc.sync.dma_start(out=bias_rows[1:2, 0 : 2 * H], in_=bhh[:, 0 : 2 * H])
+        nc.sync.dma_start(out=bias_rows[1:2, 3 * H : 4 * H], in_=bhh[:, 2 * H : 3 * H])
+
+        load_planes(nc, state_planes, gru_Whh_scales)
+        for j in range(INPUT_GROUPS // PLANES_PER_TILE):
+            load_planes(
+                nc,
+                input_planes[j],
+                gru_Wih_scales[PLANES_PER_TILE * j : PLANES_PER_TILE * (j + 1), :, :],
+            )
+
+        x_words = x_sb[:].bitcast(F32)
+        x_codes = keep.tile([P, GROUPS * P], U32, align_bytes=64)
+        x_planes = keep.tile([P, GROUPS * P], U8, align_bytes=64)
+
+        def quantise(rnd, grouped):
+            cols = slice(ROUND_GROUPS * P * rnd, ROUND_GROUPS * P * (rnd + 1))
+            nc.vector.quantize_mx(
+                out=x_codes[:, cols].bitcast(FP8X4), scales=x_planes[:, cols], in_=grouped[:]
+            )
+
+        previous = None
+        for rnd in range(GROUPS // ROUND_GROUPS):
+            xt = psum_work.tile([P, 2 * ROUND_GROUPS, P], F32, tag="work")
+            for s in range(2 * ROUND_GROUPS):
+                g = ROUND_GROUPS * rnd + s // 2
+                u = s % 2
+                nc.tensor.transpose(
+                    xt[:, s, :],
+                    x_words[:, GROUP_WORDS * g + u : GROUP_WORDS * (g + 1) : 2],
+                    identity[:],
+                )
+            grouped = stage.tile([P, ROUND_GROUPS * K_PASS], BF16, align_bytes=64)
+            nc.scalar.copy(
+                out=grouped[:].bitcast(F32).rearrange("p (g r u) -> p g r u", g=ROUND_GROUPS, u=2),
+                in_=xt[:].rearrange("p (g u) r -> p g r u", u=2),
+            )
+            if previous is not None:
+                quantise(rnd - 1, previous)
+            previous = grouped
+        quantise(GROUPS // ROUND_GROUPS - 1, previous)
+
+        bias = keep.tile([P, (GATES + 1) * H], F32)
+        for c in range((GATES + 1) * H // BANK):
+            cols = slice(BANK * c, BANK * (c + 1))
+            spread = psum_work.tile([P, BANK], F32, tag="work")
+            nc.tensor.matmul(spread[:], lhsT=ones[:], rhs=bias_rows[:, cols], start=True, stop=True)
+            nc.vector.tensor_copy(out=bias[:, cols], in_=spread[:])
+
+        def mx_passes(sums, group, words, planes, slot, first_col, start, stop):
+            x_cols = slice(P * group, P * (group + 1))
+            for c, bank in enumerate(sums):
+                nc.tensor.matmul_mx(
+                    out=bank[:],
+                    lhsT=x_codes[:, x_cols].bitcast(FP8X4),
+                    lhsT_scale=x_planes[:, x_cols],
+                    rhs=words[:, BANK * c : BANK * (c + 1)].bitcast(FP8X4),
+                    rhs_scale=planes[
+                        PACK * slot : P, first_col + BANK * c : first_col + BANK * (c + 1)
+                    ],
+                    start=start,
+                    stop=stop,
+                )
+
+        sums_rz = [
+            psum_rz.tile([P, BANK], F32, name="sums_rz%d" % c) for c in range(2 * H // BANK)
+        ]
+        sums_hn = [
+            psum_work.tile([P, BANK], F32, name="sums_hn%d" % c, tag="work")
+            for c in range(H // BANK)
+        ]
+
+        for g in range(STATE_GROUPS):
+            words = w_state.tile([P, GATES * H], U32, align_bytes=64)
+            nc.sync.dma_start(
+                out=words[:].bitcast(I32),
+                in_=gru_Whh_words[g].rearrange("p n t -> p (n t)").bitcast(I32),
+            )
+            mx_passes(sums_rz, g, words[:, 0 : 2 * H], state_planes, g, 0, g == 0, False)
+            mx_passes(
+                sums_hn,
+                g,
+                words[:, 2 * H : 3 * H],
+                state_planes,
+                g,
+                2 * H,
+                g == 0,
+                g == STATE_GROUPS - 1,
+            )
+
+        gh_n = keep.tile([P, H], F32)
+        for c in range(H // BANK):
+            cols = slice(BANK * c, BANK * (c + 1))
+            nc.vector.tensor_tensor(
+                out=gh_n[:, cols],
+                in0=sums_hn[c][:],
+                in1=bias[:, 3 * H + BANK * c : 3 * H + BANK * (c + 1)],
+                op=ALU.add,
+            )
+
+        for g in range(INPUT_GROUPS):
+            words = w_gates.tile([P, 2 * H], U32, align_bytes=64)
+            nc.sync.dma_start(
+                out=words[:].bitcast(I32),
+                in_=gru_Wih_words[g]
+                .rearrange("p n t -> p (n t)")[:, 0 : 2 * H * PACK]
+                .bitcast(I32),
+            )
+            mx_passes(
+                sums_rz,
+                STATE_GROUPS + g,
+                words,
+                input_planes[g // PLANES_PER_TILE],
+                g % PLANES_PER_TILE,
+                0,
+                False,
+                g == INPUT_GROUPS - 1,
+            )
+
+        gates = keep.tile([P, 2 * H], F32)
+        for c in range(2 * H // BANK):
+            cols = slice(BANK * c, BANK * (c + 1))
+            nc.vector.tensor_tensor(
+                out=gates[:, cols], in0=sums_rz[c][:], in1=bias[:, cols], op=ALU.add
+            )
+            nc.scalar.activation(out=gates[:, cols], in_=gates[:, cols], func=ACT.Sigmoid)
+        r = gates[:, 0:H]
+        z = gates[:, H : 2 * H]
+        r_gh_n = keep.tile([P, H], F32)
+        nc.vector.tensor_tensor(out=r_gh_n[:], in0=r, in1=gh_n[:], op=ALU.mult)
+        z_state = keep.tile([P, H], F32)
+        nc.vector.tensor_tensor(out=z_state[:], in0=z, in1=x_sb[:, 0:H], op=ALU.mult)
+        addend = keep.tile([P, H], F32)
+        nc.vector.tensor_tensor(
+            out=addend[:], in0=r_gh_n[:], in1=bias[:, 2 * H : 3 * H], op=ALU.add
+        )
+        one_minus_z = keep.tile([P, H], F32)
+        nc.vector.tensor_scalar(
+            out=one_minus_z[:], in0=z, scalar1=-1.0, scalar2=1.0, op0=ALU.mult, op1=ALU.add
+        )
+
+        sums_in = [
+            psum_work.tile([P, BANK], F32, name="sums_in%d" % c, tag="work")
+            for c in range(H // BANK)
+        ]
+        for g in range(INPUT_GROUPS):
+            words = w_cand.tile([P, H], U32, align_bytes=64)
+            nc.sync.dma_start(
+                out=words[:].bitcast(I32),
+                in_=gru_Wih_words[g]
+                .rearrange("p n t -> p (n t)")[:, 2 * H * PACK : 3 * H * PACK]
+                .bitcast(I32),
+            )
+            mx_passes(
+                sums_in,
+                STATE_GROUPS + g,
+                words,
+                input_planes[g // PLANES_PER_TILE],
+                g % PLANES_PER_TILE,
+                2 * H,
+                g == 0,
+                g == INPUT_GROUPS - 1,
+            )
+
+        halves = [slice(BANK * c, BANK * (c + 1)) for c in range(H // BANK)]
+        belief = keep.tile([P, H], F32)
+        for c, cols in enumerate(halves):
+            nc.vector.tensor_tensor(
+                out=belief[:, cols], in0=sums_in[c][:], in1=addend[:, cols], op=ALU.add
+            )
+            nc.scalar.activation(out=belief[:, cols], in_=belief[:, cols], func=ACT.Tanh)
+        for cols in halves:
+            nc.vector.tensor_tensor(
+                out=belief[:, cols], in0=belief[:, cols], in1=one_minus_z[:, cols], op=ALU.mult
+            )
+        for cols in halves:
+            nc.vector.tensor_tensor(
+                out=belief[:, cols], in0=belief[:, cols], in1=z_state[:, cols], op=ALU.add
+            )
+            nc.sync.dma_start(out=out[:, cols], in_=belief[:, cols])

@@ -36,9 +36,9 @@ def load_planes(nc, planes, scales):
     groups = scales.shape[0]
     for quadrant in range(P // QUADRANT):
         first = QUADRANT * quadrant
-        nc.sync.dma_start(
-            out=planes[first : first + PACK * groups, :].bitcast(I32),
-            in_=scales[:, PACK * quadrant : PACK * (quadrant + 1), :].bitcast(I32),
+        nc.gpsimd.dma_start(
+            out=planes[first : first + PACK * groups, :].bitcast(F32),
+            in_=scales[:, PACK * quadrant : PACK * (quadrant + 1), :].bitcast(F32),
         )
 
 
@@ -66,19 +66,23 @@ def tile_rssm_pb_k_kernel(
         psum_rz = ctx.enter_context(tc.psum_pool(name="psum_rz", bufs=1))
         psum_work = ctx.enter_context(tc.psum_pool(name="psum_work", bufs=4))
 
-        bias_rows = keep.tile([P, (GATES + 1) * H], BF16)
-        nc.vector.memset(bias_rows[:], 0.0)
-        ones = keep.tile([P, P], BF16)
-        nc.vector.memset(ones[:], 1.0)
         identity = keep.tile([P, P], F32)
         make_identity(nc, identity[:])
         state_planes = keep.tile([P, GATES * H], U8, align_bytes=64)
         nc.vector.memset(state_planes[:].bitcast(I32), 0)
+        load_planes(nc, state_planes, gru_Whh_scales)
         input_planes = []
         for j in range(INPUT_GROUPS // PLANES_PER_TILE):
             planes = keep.tile([P, GATES * H], U8, name="input_planes%d" % j, align_bytes=64)
             nc.vector.memset(planes[:].bitcast(I32), 0)
+            load_planes(
+                nc, planes, gru_Wih_scales[PLANES_PER_TILE * j : PLANES_PER_TILE * (j + 1), :, :]
+            )
             input_planes.append(planes)
+        bias_rows = keep.tile([P, (GATES + 1) * H], BF16)
+        nc.vector.memset(bias_rows[:], 0.0)
+        ones = keep.tile([P, P], BF16)
+        nc.vector.memset(ones[:], 1.0)
 
         x_sb = keep.tile([P, X_COLS], BF16)
         nc.sync.dma_start(out=x_sb[:, 0:H], in_=prev_state)
@@ -92,14 +96,6 @@ def tile_rssm_pb_k_kernel(
         nc.sync.dma_start(out=bias_rows[0:1, 0 : 3 * H], in_=bih)
         nc.sync.dma_start(out=bias_rows[1:2, 0 : 2 * H], in_=bhh[:, 0 : 2 * H])
         nc.sync.dma_start(out=bias_rows[1:2, 3 * H : 4 * H], in_=bhh[:, 2 * H : 3 * H])
-
-        load_planes(nc, state_planes, gru_Whh_scales)
-        for j in range(INPUT_GROUPS // PLANES_PER_TILE):
-            load_planes(
-                nc,
-                input_planes[j],
-                gru_Wih_scales[PLANES_PER_TILE * j : PLANES_PER_TILE * (j + 1), :, :],
-            )
 
         x_words = x_sb[:].bitcast(F32)
         x_codes = keep.tile([P, GROUPS * P], U32, align_bytes=64)

@@ -28,6 +28,8 @@ PLANES_PER_TILE = 4
 QUADRANT = 32
 GROUP_WORDS = K_PASS // 2
 ROUND_GROUPS = 2
+SLICE = 256
+SLICED_GROUPS = 4
 
 FLOPS = 2 * P * GROUPS * K_PASS * GATES * H
 
@@ -36,9 +38,9 @@ def load_planes(nc, planes, scales):
     groups = scales.shape[0]
     for quadrant in range(P // QUADRANT):
         first = QUADRANT * quadrant
-        nc.gpsimd.dma_start(
-            out=planes[first : first + PACK * groups, :].bitcast(F32),
-            in_=scales[:, PACK * quadrant : PACK * (quadrant + 1), :].bitcast(F32),
+        nc.sync.dma_start(
+            out=planes[first : first + PACK * groups, :].bitcast(I32),
+            in_=scales[:, PACK * quadrant : PACK * (quadrant + 1), :].bitcast(I32),
         )
 
 
@@ -66,8 +68,6 @@ def tile_rssm_pb_k_kernel(
         psum_rz = ctx.enter_context(tc.psum_pool(name="psum_rz", bufs=1))
         psum_work = ctx.enter_context(tc.psum_pool(name="psum_work", bufs=4))
 
-        identity = keep.tile([P, P], F32)
-        make_identity(nc, identity[:])
         state_planes = keep.tile([P, GATES * H], U8, align_bytes=64)
         nc.vector.memset(state_planes[:].bitcast(I32), 0)
         load_planes(nc, state_planes, gru_Whh_scales)
@@ -83,6 +83,8 @@ def tile_rssm_pb_k_kernel(
         nc.vector.memset(bias_rows[:], 0.0)
         ones = keep.tile([P, P], BF16)
         nc.vector.memset(ones[:], 1.0)
+        identity = keep.tile([P, P], F32)
+        make_identity(nc, identity[:])
 
         x_sb = keep.tile([P, X_COLS], BF16)
         nc.sync.dma_start(out=x_sb[:, 0:H], in_=prev_state)
@@ -138,13 +140,14 @@ def tile_rssm_pb_k_kernel(
         def mx_passes(sums, group, words, planes, slot, first_col, start, stop):
             x_cols = slice(P * group, P * (group + 1))
             for c, bank in enumerate(sums):
+                width = bank.shape[1]
                 nc.tensor.matmul_mx(
                     out=bank[:],
                     lhsT=x_codes[:, x_cols].bitcast(FP8X4),
                     lhsT_scale=x_planes[:, x_cols],
-                    rhs=words[:, BANK * c : BANK * (c + 1)].bitcast(FP8X4),
+                    rhs=words[:, width * c : width * (c + 1)].bitcast(FP8X4),
                     rhs_scale=planes[
-                        PACK * slot : P, first_col + BANK * c : first_col + BANK * (c + 1)
+                        PACK * slot : P, first_col + width * c : first_col + width * (c + 1)
                     ],
                     start=start,
                     stop=stop,
@@ -228,10 +231,11 @@ def tile_rssm_pb_k_kernel(
         )
 
         sums_in = [
-            psum_work.tile([P, BANK], F32, name="sums_in%d" % c, tag="work")
-            for c in range(H // BANK)
+            psum_work.tile([P, SLICE], F32, name="sums_in%d" % s, tag="work")
+            for s in range(H // SLICE)
         ]
-        for g in range(INPUT_GROUPS):
+        whole_groups = INPUT_GROUPS - SLICED_GROUPS
+        for g in range(whole_groups):
             words = w_cand.tile([P, H], U32, align_bytes=64)
             nc.sync.dma_start(
                 out=words[:].bitcast(I32),
@@ -247,22 +251,54 @@ def tile_rssm_pb_k_kernel(
                 g % PLANES_PER_TILE,
                 2 * H,
                 g == 0,
-                g == INPUT_GROUPS - 1,
+                False,
             )
 
-        halves = [slice(BANK * c, BANK * (c + 1)) for c in range(H // BANK)]
         belief = keep.tile([P, H], F32)
-        for c, cols in enumerate(halves):
+
+        def candidate(s):
+            cols = slice(SLICE * s, SLICE * (s + 1))
             nc.vector.tensor_tensor(
-                out=belief[:, cols], in0=sums_in[c][:], in1=addend[:, cols], op=ALU.add
+                out=belief[:, cols], in0=sums_in[s][:], in1=addend[:, cols], op=ALU.add
             )
             nc.scalar.activation(out=belief[:, cols], in_=belief[:, cols], func=ACT.Tanh)
-        for cols in halves:
+
+        def blend_and_store(s):
+            cols = slice(SLICE * s, SLICE * (s + 1))
             nc.vector.tensor_tensor(
                 out=belief[:, cols], in0=belief[:, cols], in1=one_minus_z[:, cols], op=ALU.mult
             )
-        for cols in halves:
             nc.vector.tensor_tensor(
                 out=belief[:, cols], in0=belief[:, cols], in1=z_state[:, cols], op=ALU.add
             )
             nc.sync.dma_start(out=out[:, cols], in_=belief[:, cols])
+
+        slices = []
+        for s in range(H // SLICE):
+            first_col = 2 * H + SLICE * s
+            sliced = w_cand.tile([P, SLICED_GROUPS, SLICE], U32, tag="words", align_bytes=64)
+            nc.sync.dma_start(
+                out=sliced[:].bitcast(I32),
+                in_=gru_Wih_words[whole_groups:INPUT_GROUPS, :, first_col : first_col + SLICE, :]
+                .rearrange("g p n t -> p g (n t)")
+                .bitcast(I32),
+            )
+            slices.append(sliced)
+
+        for s in range(H // SLICE):
+            for i in range(SLICED_GROUPS):
+                g = whole_groups + i
+                mx_passes(
+                    sums_in[s : s + 1],
+                    STATE_GROUPS + g,
+                    slices[s][:, i, :],
+                    input_planes[g // PLANES_PER_TILE],
+                    g % PLANES_PER_TILE,
+                    2 * H + SLICE * s,
+                    False,
+                    i == SLICED_GROUPS - 1,
+                )
+            candidate(s)
+            if s > 0:
+                blend_and_store(s - 1)
+        blend_and_store(H // SLICE - 1)

@@ -68,17 +68,24 @@ def tile_rssm_pb_k_kernel(
         psum_rz = ctx.enter_context(tc.psum_pool(name="psum_rz", bufs=1))
         psum_work = ctx.enter_context(tc.psum_pool(name="psum_work", bufs=4))
 
-        state_planes = keep.tile([P, GATES * H], U8, align_bytes=64)
-        nc.vector.memset(state_planes[:].bitcast(I32), 0)
-        load_planes(nc, state_planes, gru_Whh_scales)
         input_planes = []
         for j in range(INPUT_GROUPS // PLANES_PER_TILE):
             planes = keep.tile([P, GATES * H], U8, name="input_planes%d" % j, align_bytes=64)
-            nc.vector.memset(planes[:].bitcast(I32), 0)
-            load_planes(
-                nc, planes, gru_Wih_scales[PLANES_PER_TILE * j : PLANES_PER_TILE * (j + 1), :, :]
-            )
             input_planes.append(planes)
+        filled_tiles = INPUT_GROUPS // PLANES_PER_TILE - 1
+        for j in range(filled_tiles):
+            load_planes(
+                nc,
+                input_planes[j],
+                gru_Wih_scales[PLANES_PER_TILE * j : PLANES_PER_TILE * (j + 2), :, :],
+            )
+        state_planes = keep.tile([P, GATES * H], U8, align_bytes=64)
+        nc.vector.memset(state_planes[:].bitcast(I32), 0)
+        load_planes(nc, state_planes, gru_Whh_scales)
+        nc.vector.memset(input_planes[filled_tiles][:].bitcast(I32), 0)
+        load_planes(
+            nc, input_planes[filled_tiles], gru_Wih_scales[PLANES_PER_TILE * filled_tiles :, :, :]
+        )
         bias_rows = keep.tile([P, (GATES + 1) * H], BF16)
         nc.vector.memset(bias_rows[:], 0.0)
         ones = keep.tile([P, P], BF16)

@@ -30,6 +30,7 @@ GROUP_WORDS = K_PASS // 2
 ROUND_GROUPS = 2
 SLICE = 256
 SLICED_GROUPS = 4
+LOAD_GROUPS = 4
 
 FLOPS = 2 * P * GROUPS * K_PASS * GATES * H
 
@@ -62,9 +63,8 @@ def tile_rssm_pb_k_kernel(
         ctx.enter_context(tc.manual_schedule())
         keep = ctx.enter_context(tc.tile_pool(name="keep", bufs=1))
         stage = ctx.enter_context(tc.tile_pool(name="stage", bufs=3))
-        w_state = ctx.enter_context(tc.tile_pool(name="w_state", bufs=2))
-        w_gates = ctx.enter_context(tc.tile_pool(name="w_gates", bufs=6))
-        w_cand = ctx.enter_context(tc.tile_pool(name="w_cand", bufs=8))
+        w_big = ctx.enter_context(tc.tile_pool(name="w_big", bufs=3))
+        w_cand = ctx.enter_context(tc.tile_pool(name="w_cand", bufs=4))
         psum_rz = ctx.enter_context(tc.psum_pool(name="psum_rz", bufs=1))
         psum_work = ctx.enter_context(tc.psum_pool(name="psum_work", bufs=4))
 
@@ -168,17 +168,17 @@ def tile_rssm_pb_k_kernel(
             for c in range(H // BANK)
         ]
 
+        state_words = w_big.tile([P, STATE_GROUPS, GATES * H], U32, tag="words", align_bytes=64)
+        nc.sync.dma_start(
+            out=state_words[:].bitcast(I32),
+            in_=gru_Whh_words.rearrange("g p n t -> p g (n t)").bitcast(I32),
+        )
         for g in range(STATE_GROUPS):
-            words = w_state.tile([P, GATES * H], U32, align_bytes=64)
-            nc.sync.dma_start(
-                out=words[:].bitcast(I32),
-                in_=gru_Whh_words[g].rearrange("p n t -> p (n t)").bitcast(I32),
-            )
-            mx_passes(sums_rz, g, words[:, 0 : 2 * H], state_planes, g, 0, g == 0, False)
+            mx_passes(sums_rz, g, state_words[:, g, 0 : 2 * H], state_planes, g, 0, g == 0, False)
             mx_passes(
                 sums_hn,
                 g,
-                words[:, 2 * H : 3 * H],
+                state_words[:, g, 2 * H : 3 * H],
                 state_planes,
                 g,
                 2 * H,
@@ -197,17 +197,18 @@ def tile_rssm_pb_k_kernel(
             )
 
         for g in range(INPUT_GROUPS):
-            words = w_gates.tile([P, 2 * H], U32, align_bytes=64)
-            nc.sync.dma_start(
-                out=words[:].bitcast(I32),
-                in_=gru_Wih_words[g]
-                .rearrange("p n t -> p (n t)")[:, 0 : 2 * H * PACK]
-                .bitcast(I32),
-            )
+            if g % LOAD_GROUPS == 0:
+                words = w_big.tile([P, LOAD_GROUPS, 2 * H], U32, tag="words", align_bytes=64)
+                nc.sync.dma_start(
+                    out=words[:].bitcast(I32),
+                    in_=gru_Wih_words[g : g + LOAD_GROUPS, :, 0 : 2 * H, :]
+                    .rearrange("g p n t -> p g (n t)")
+                    .bitcast(I32),
+                )
             mx_passes(
                 sums_rz,
                 STATE_GROUPS + g,
-                words,
+                words[:, g % LOAD_GROUPS, :],
                 input_planes[g // PLANES_PER_TILE],
                 g % PLANES_PER_TILE,
                 0,
@@ -243,17 +244,18 @@ def tile_rssm_pb_k_kernel(
         ]
         whole_groups = INPUT_GROUPS - SLICED_GROUPS
         for g in range(whole_groups):
-            words = w_cand.tile([P, H], U32, align_bytes=64)
-            nc.sync.dma_start(
-                out=words[:].bitcast(I32),
-                in_=gru_Wih_words[g]
-                .rearrange("p n t -> p (n t)")[:, 2 * H * PACK : 3 * H * PACK]
-                .bitcast(I32),
-            )
+            if g % LOAD_GROUPS == 0:
+                words = w_big.tile([P, LOAD_GROUPS, H], U32, tag="words", align_bytes=64)
+                nc.sync.dma_start(
+                    out=words[:].bitcast(I32),
+                    in_=gru_Wih_words[g : g + LOAD_GROUPS, :, 2 * H : 3 * H, :]
+                    .rearrange("g p n t -> p g (n t)")
+                    .bitcast(I32),
+                )
             mx_passes(
                 sums_in,
                 STATE_GROUPS + g,
-                words,
+                words[:, g % LOAD_GROUPS, :],
                 input_planes[g // PLANES_PER_TILE],
                 g % PLANES_PER_TILE,
                 2 * H,

@@ -31,6 +31,7 @@ ROUND_GROUPS = 2
 SLICE = 256
 SLICED_GROUPS = 4
 LOAD_GROUPS = 4
+SINGLE_GROUPS = 4
 
 FLOPS = 2 * P * GROUPS * K_PASS * GATES * H
 
@@ -64,7 +65,7 @@ def tile_rssm_pb_k_kernel(
         keep = ctx.enter_context(tc.tile_pool(name="keep", bufs=1))
         stage = ctx.enter_context(tc.tile_pool(name="stage", bufs=3))
         w_big = ctx.enter_context(tc.tile_pool(name="w_big", bufs=3))
-        w_cand = ctx.enter_context(tc.tile_pool(name="w_cand", bufs=4))
+        w_cand = ctx.enter_context(tc.tile_pool(name="w_cand", bufs=5))
         psum_rz = ctx.enter_context(tc.psum_pool(name="psum_rz", bufs=1))
         psum_work = ctx.enter_context(tc.psum_pool(name="psum_work", bufs=4))
 
@@ -244,18 +245,29 @@ def tile_rssm_pb_k_kernel(
         ]
         whole_groups = INPUT_GROUPS - SLICED_GROUPS
         for g in range(whole_groups):
-            if g % LOAD_GROUPS == 0:
-                words = w_big.tile([P, LOAD_GROUPS, H], U32, tag="words", align_bytes=64)
+            if g >= whole_groups - SINGLE_GROUPS:
+                single = w_cand.tile([P, H], U32, tag="words", align_bytes=64)
                 nc.sync.dma_start(
-                    out=words[:].bitcast(I32),
-                    in_=gru_Wih_words[g : g + LOAD_GROUPS, :, 2 * H : 3 * H, :]
-                    .rearrange("g p n t -> p g (n t)")
+                    out=single[:].bitcast(I32),
+                    in_=gru_Wih_words[g]
+                    .rearrange("p n t -> p (n t)")[:, 2 * H * PACK : 3 * H * PACK]
                     .bitcast(I32),
                 )
+                group_words = single[:, :]
+            else:
+                if g % LOAD_GROUPS == 0:
+                    words = w_big.tile([P, LOAD_GROUPS, H], U32, tag="words", align_bytes=64)
+                    nc.sync.dma_start(
+                        out=words[:].bitcast(I32),
+                        in_=gru_Wih_words[g : g + LOAD_GROUPS, :, 2 * H : 3 * H, :]
+                        .rearrange("g p n t -> p g (n t)")
+                        .bitcast(I32),
+                    )
+                group_words = words[:, g % LOAD_GROUPS, :]
             mx_passes(
                 sums_in,
                 STATE_GROUPS + g,
-                words[:, g % LOAD_GROUPS, :],
+                group_words,
                 input_planes[g // PLANES_PER_TILE],
                 g % PLANES_PER_TILE,
                 2 * H,

from contextlib import ExitStack

import concourse.mybir as mybir
from concourse.masks import make_identity

F32 = mybir.dt.float32
BF16 = mybir.dt.bfloat16
I32 = mybir.dt.int32
U32 = mybir.dt.uint32
U8 = mybir.dt.uint8
FP8X4 = mybir.dt.float8_e4m3fn_x4
ACT = mybir.ActivationFunctionType
ALU = mybir.AluOpType

P = 128
PACK = 4
K_PASS = P * PACK
BANK = 512
H = 1024
GATES = 3
SAMPLE = 8064
STATE_GROUPS = 2
INPUT_GROUPS = 16
GROUPS = STATE_GROUPS + INPUT_GROUPS
X_COLS = GROUPS * K_PASS
X_PIECE = 2048
PLANES_PER_TILE = 4
QUADRANT = 32
GROUP_WORDS = K_PASS // 2
ROUND_GROUPS = 2
SLICE = 256
SLICED_GROUPS = 4
LOAD_GROUPS = 4
SINGLE_GROUPS = 4

FLOPS = 2 * P * GROUPS * K_PASS * GATES * H


def load_planes(nc, planes, scales):
    groups = scales.shape[0]
    for quadrant in range(P // QUADRANT):
        first = QUADRANT * quadrant
        nc.sync.dma_start(
            out=planes[first : first + PACK * groups, :].bitcast(I32),
            in_=scales[:, PACK * quadrant : PACK * (quadrant + 1), :].bitcast(I32),
        )


def tile_rssm_pb_k_kernel(
    tc,
    sample,
    prev_action,
    prev_state,
    gru_Wih_words,
    gru_Wih_scales,
    gru_Whh_words,
    gru_Whh_scales,
    gru_bih,
    gru_bhh,
    out,
):
    nc = tc.nc
    with ExitStack() as ctx:
        ctx.enter_context(tc.manual_schedule())
        keep = ctx.enter_context(tc.tile_pool(name="keep", bufs=1))
        stage = ctx.enter_context(tc.tile_pool(name="stage", bufs=3))
        w_big = ctx.enter_context(tc.tile_pool(name="w_big", bufs=3))
        w_cand = ctx.enter_context(tc.tile_pool(name="w_cand", bufs=5))
        psum_rz = ctx.enter_context(tc.psum_pool(name="psum_rz", bufs=1))
        psum_work = ctx.enter_context(tc.psum_pool(name="psum_work", bufs=4))

        input_planes = []
        for j in range(INPUT_GROUPS // PLANES_PER_TILE):
            planes = keep.tile([P, GATES * H], U8, name="input_planes%d" % j, align_bytes=64)
            input_planes.append(planes)
        filled_tiles = INPUT_GROUPS // PLANES_PER_TILE - 1
        for j in range(filled_tiles):
            load_planes(
                nc,
                input_planes[j],
                gru_Wih_scales[PLANES_PER_TILE * j : PLANES_PER_TILE * (j + 2), :, :],
            )
        state_planes = keep.tile([P, GATES * H], U8, align_bytes=64)
        nc.vector.memset(state_planes[:].bitcast(I32), 0)
        load_planes(nc, state_planes, gru_Whh_scales)
        nc.vector.memset(input_planes[filled_tiles][:].bitcast(I32), 0)
        load_planes(
            nc, input_planes[filled_tiles], gru_Wih_scales[PLANES_PER_TILE * filled_tiles :, :, :]
        )
        bias_rows = keep.tile([P, (GATES + 1) * H], BF16)
        nc.vector.memset(bias_rows[:], 0.0)
        ones = keep.tile([P, P], BF16)
        nc.vector.memset(ones[:], 1.0)
        identity = keep.tile([P, P], F32)
        make_identity(nc, identity[:])

        x_sb = keep.tile([P, X_COLS], BF16)
        nc.sync.dma_start(out=x_sb[:, 0:H], in_=prev_state)
        for first in range(0, SAMPLE, X_PIECE):
            last = min(first + X_PIECE, SAMPLE)
            nc.sync.dma_start(out=x_sb[:, H + first : H + last], in_=sample[:, first:last])
        nc.sync.dma_start(out=x_sb[:, H + SAMPLE : X_COLS], in_=prev_action)

        bih = gru_bih.rearrange("(o n) -> o n", o=1)
        bhh = gru_bhh.rearrange("(o n) -> o n", o=1)
        nc.sync.dma_start(out=bias_rows[0:1, 0 : 3 * H], in_=bih)
        nc.sync.dma_start(out=bias_rows[1:2, 0 : 2 * H], in_=bhh[:, 0 : 2 * H])
        nc.sync.dma_start(out=bias_rows[1:2, 3 * H : 4 * H], in_=bhh[:, 2 * H : 3 * H])

        x_words = x_sb[:].bitcast(F32)
        x_codes = keep.tile([P, GROUPS * P], U32, align_bytes=64)
        x_planes = keep.tile([P, GROUPS * P], U8, align_bytes=64)

        def quantise(rnd, grouped):
            cols = slice(ROUND_GROUPS * P * rnd, ROUND_GROUPS * P * (rnd + 1))
            nc.vector.quantize_mx(
                out=x_codes[:, cols].bitcast(FP8X4), scales=x_planes[:, cols], in_=grouped[:]
            )

        previous = None
        for rnd in range(GROUPS // ROUND_GROUPS):
            xt = psum_work.tile([P, 2 * ROUND_GROUPS, P], F32, tag="work")
            for s in range(2 * ROUND_GROUPS):
                g = ROUND_GROUPS * rnd + s // 2
                u = s % 2
                nc.tensor.transpose(
                    xt[:, s, :],
                    x_words[:, GROUP_WORDS * g + u : GROUP_WORDS * (g + 1) : 2],
                    identity[:],
                )
            grouped = stage.tile([P, ROUND_GROUPS * K_PASS], BF16, align_bytes=64)
            nc.scalar.copy(
                out=grouped[:].bitcast(F32).rearrange("p (g r u) -> p g r u", g=ROUND_GROUPS, u=2),
                in_=xt[:].rearrange("p (g u) r -> p g r u", u=2),
            )
            if previous is not None:
                quantise(rnd - 1, previous)
            previous = grouped
        quantise(GROUPS // ROUND_GROUPS - 1, previous)

        bias = keep.tile([P, (GATES + 1) * H], F32)
        for c in range((GATES + 1) * H // BANK):
            cols = slice(BANK * c, BANK * (c + 1))
            spread = psum_work.tile([P, BANK], F32, tag="work")
            nc.tensor.matmul(spread[:], lhsT=ones[:], rhs=bias_rows[:, cols], start=True, stop=True)
            nc.vector.tensor_copy(out=bias[:, cols], in_=spread[:])

        def mx_passes(sums, group, words, planes, slot, first_col, start, stop):
            x_cols = slice(P * group, P * (group + 1))
            for c, bank in enumerate(sums):
                width = bank.shape[1]
                nc.tensor.matmul_mx(
                    out=bank[:],
                    lhsT=x_codes[:, x_cols].bitcast(FP8X4),
                    lhsT_scale=x_planes[:, x_cols],
                    rhs=words[:, width * c : width * (c + 1)].bitcast(FP8X4),
                    rhs_scale=planes[
                        PACK * slot : P, first_col + width * c : first_col + width * (c + 1)
                    ],
                    start=start,
                    stop=stop,
                )

        sums_rz = [
            psum_rz.tile([P, BANK], F32, name="sums_rz%d" % c) for c in range(2 * H // BANK)
        ]
        sums_hn = [
            psum_work.tile([P, BANK], F32, name="sums_hn%d" % c, tag="work")
            for c in range(H // BANK)
        ]

        state_words = w_big.tile([P, STATE_GROUPS, GATES * H], U32, tag="words", align_bytes=64)
        nc.sync.dma_start(
            out=state_words[:].bitcast(I32),
            in_=gru_Whh_words.rearrange("g p n t -> p g (n t)").bitcast(I32),
        )
        for g in range(STATE_GROUPS):
            mx_passes(sums_rz, g, state_words[:, g, 0 : 2 * H], state_planes, g, 0, g == 0, False)
            mx_passes(
                sums_hn,
                g,
                state_words[:, g, 2 * H : 3 * H],
                state_planes,
                g,
                2 * H,
                g == 0,
                g == STATE_GROUPS - 1,
            )

        gh_n = keep.tile([P, H], F32)
        for c in range(H // BANK):
            cols = slice(BANK * c, BANK * (c + 1))
            nc.vector.tensor_tensor(
                out=gh_n[:, cols],
                in0=sums_hn[c][:],
                in1=bias[:, 3 * H + BANK * c : 3 * H + BANK * (c + 1)],
                op=ALU.add,
            )

        for g in range(INPUT_GROUPS):
            if g % LOAD_GROUPS == 0:
                words = w_big.tile([P, LOAD_GROUPS, 2 * H], U32, tag="words", align_bytes=64)
                nc.sync.dma_start(
                    out=words[:].bitcast(I32),
                    in_=gru_Wih_words[g : g + LOAD_GROUPS, :, 0 : 2 * H, :]
                    .rearrange("g p n t -> p g (n t)")
                    .bitcast(I32),
                )
            mx_passes(
                sums_rz,
                STATE_GROUPS + g,
                words[:, g % LOAD_GROUPS, :],
                input_planes[g // PLANES_PER_TILE],
                g % PLANES_PER_TILE,
                0,
                False,
                g == INPUT_GROUPS - 1,
            )

        gates = keep.tile([P, 2 * H], F32)
        for c in range(2 * H // BANK):
            cols = slice(BANK * c, BANK * (c + 1))
            nc.vector.tensor_tensor(
                out=gates[:, cols], in0=sums_rz[c][:], in1=bias[:, cols], op=ALU.add
            )
            nc.scalar.activation(out=gates[:, cols], in_=gates[:, cols], func=ACT.Sigmoid)
        r = gates[:, 0:H]
        z = gates[:, H : 2 * H]
        r_gh_n = keep.tile([P, H], F32)
        nc.vector.tensor_tensor(out=r_gh_n[:], in0=r, in1=gh_n[:], op=ALU.mult)
        z_state = keep.tile([P, H], F32)
        nc.vector.tensor_tensor(out=z_state[:], in0=z, in1=x_sb[:, 0:H], op=ALU.mult)
        addend = keep.tile([P, H], F32)
        nc.vector.tensor_tensor(
            out=addend[:], in0=r_gh_n[:], in1=bias[:, 2 * H : 3 * H], op=ALU.add
        )
        one_minus_z = keep.tile([P, H], F32)
        nc.vector.tensor_scalar(
            out=one_minus_z[:], in0=z, scalar1=-1.0, scalar2=1.0, op0=ALU.mult, op1=ALU.add
        )

        sums_in = [
            psum_work.tile([P, SLICE], F32, name="sums_in%d" % s, tag="work")
            for s in range(H // SLICE)
        ]
        whole_groups = INPUT_GROUPS - SLICED_GROUPS
        for g in range(whole_groups):
            if g >= whole_groups - SINGLE_GROUPS:
                single = w_cand.tile([P, H], U32, tag="words", align_bytes=64)
                nc.sync.dma_start(
                    out=single[:].bitcast(I32),
                    in_=gru_Wih_words[g]
                    .rearrange("p n t -> p (n t)")[:, 2 * H * PACK : 3 * H * PACK]
                    .bitcast(I32),
                )
                group_words = single[:, :]
            else:
                if g % LOAD_GROUPS == 0:
                    words = w_big.tile([P, LOAD_GROUPS, H], U32, tag="words", align_bytes=64)
                    nc.sync.dma_start(
                        out=words[:].bitcast(I32),
                        in_=gru_Wih_words[g : g + LOAD_GROUPS, :, 2 * H : 3 * H, :]
                        .rearrange("g p n t -> p g (n t)")
                        .bitcast(I32),
                    )
                group_words = words[:, g % LOAD_GROUPS, :]
            mx_passes(
                sums_in,
                STATE_GROUPS + g,
                group_words,
                input_planes[g // PLANES_PER_TILE],
                g % PLANES_PER_TILE,
                2 * H,
                g == 0,
                False,
            )

        belief = keep.tile([P, H], F32)

        def candidate(s):
            cols = slice(SLICE * s, SLICE * (s + 1))
            nc.vector.tensor_tensor(
                out=belief[:, cols], in0=sums_in[s][:], in1=addend[:, cols], op=ALU.add
            )
            nc.scalar.activation(out=belief[:, cols], in_=belief[:, cols], func=ACT.Tanh)

        def blend_and_store(s):
            cols = slice(SLICE * s, SLICE * (s + 1))
            nc.vector.tensor_tensor(
                out=belief[:, cols], in0=belief[:, cols], in1=one_minus_z[:, cols], op=ALU.mult
            )
            nc.vector.tensor_tensor(
                out=belief[:, cols], in0=belief[:, cols], in1=z_state[:, cols], op=ALU.add
            )
            nc.sync.dma_start(out=out[:, cols], in_=belief[:, cols])

        slices = []
        for s in range(H // SLICE):
            first_col = 2 * H + SLICE * s
            sliced = w_cand.tile([P, SLICED_GROUPS, SLICE], U32, tag="words", align_bytes=64)
            nc.sync.dma_start(
                out=sliced[:].bitcast(I32),
                in_=gru_Wih_words[whole_groups:INPUT_GROUPS, :, first_col : first_col + SLICE, :]
                .rearrange("g p n t -> p g (n t)")
                .bitcast(I32),
            )
            slices.append(sliced)

        for s in range(H // SLICE):
            for i in range(SLICED_GROUPS):
                g = whole_groups + i
                mx_passes(
                    sums_in[s : s + 1],
                    STATE_GROUPS + g,
                    slices[s][:, i, :],
                    input_planes[g // PLANES_PER_TILE],
                    g % PLANES_PER_TILE,
                    2 * H + SLICE * s,
                    False,
                    i == SLICED_GROUPS - 1,
                )
            candidate(s)
            if s > 0:
                blend_and_store(s - 1)
        blend_and_store(H // SLICE - 1)
